import numpy as np
import ml_dtypes


def mxq(x, axis, fmt="e4m3"):
    dtype, down = {"e4m3": (ml_dtypes.float8_e4m3fn, 7), "e5m2": (ml_dtypes.float8_e5m2, 14)}[fmt]
    v = np.moveaxis(np.asarray(x, np.float32).astype(ml_dtypes.bfloat16).astype(np.float64), axis, -1)
    blocks = v.reshape(v.shape[:-1] + (-1, 32))
    amax = np.abs(blocks).max(-1, keepdims=True)
    byte = np.maximum(np.where(amax > 0, np.frexp(amax)[1] - 1 + 127, 0) - down, 1)
    scale = np.exp2(byte - 127.0)
    codes = (blocks / scale).astype(np.float32).astype(dtype).astype(np.float64)
    return np.moveaxis((codes * scale).reshape(v.shape), -1, axis)


WIDE = False


def mx_kscale(k):
    if not WIDE:
        return np.ones(k)
    levels = np.array([10, -10, 5, -5, 0])
    if k % 512:
        return np.exp2(np.random.permutation(np.resize(levels, k // 32))).repeat(32)
    a = np.empty((k // 512, 16))
    for p in range(k // 512):
        a[p, :8] = np.random.permutation(np.resize(levels, 8))
        for g in range(8):
            far = levels[np.abs(levels - a[p, g]) >= 10]
            a[p, g + 8] = far[np.random.randint(len(far))]
    return np.exp2(a.ravel()).repeat(32)


BF16 = ml_dtypes.bfloat16


def bf(x):
    return np.asarray(x, np.float32).astype(BF16)


def f64(x):
    return np.asarray(x).astype(np.float64)


B, S, D, H, DN, DR, DV, QL, KVL, LBLK = 4, 256, 2048, 16, 128, 64, 128, 512, 512, 64
DKV = DN + DV


def silu(v):
    return v / (1.0 + np.exp(-v))


def eta(t):
    m = t.reshape(t.shape[0], H, -1).max(-1)
    m = np.where(m == 0, 1e-6, m)
    return np.minimum(10.0 / m, 1.0)


def setup_inputs():
    s, t = mx_kscale(D), mx_kscale(KVL)
    amp = np.linspace(0.5, 1.5, S)[None, :, None]
    return {"x": bf(np.random.standard_normal((B, S, D)) * amp * s),
            "wkv_c": bf(np.random.standard_normal((KVL, D)) / np.sqrt(D) / s[None, :] * t[:, None]),
            "wkv_b": bf(np.random.standard_normal((H * DKV, KVL)) * 2.5 / np.sqrt(KVL) / t[None, :])}


def reference(x, wkv_c, wkv_b):
    kv_c = mxq(f64(x), 2, "e4m3") @ mxq(f64(wkv_c), 1, "e4m3").T
    kv = (mxq(kv_c, 2, "e4m3") @ mxq(f64(wkv_b), 1, "e4m3").T).reshape(B, S, H, DKV)
    k, v = silu(kv[..., :DN]), kv[..., DN:]
    return k * eta(k)[:, None, :, None], v

@@ -1,0 +1,360 @@
+from contextlib import ExitStack
+
+import concourse.mybir as mybir
+from concourse.masks import make_identity
+
+F32 = mybir.dt.float32
+BF16 = mybir.dt.bfloat16
+U32 = mybir.dt.uint32
+U8 = mybir.dt.uint8
+FP8X4 = mybir.dt.float8_e4m3fn_x4
+ACT = mybir.ActivationFunctionType
+ALU = mybir.AluOpType
+AX = mybir.AxisListType
+
+P = 128
+B, S, D, H, KVL = 4, 256, 2048, 16, 512
+G = D // 512
+Q = 4
+NQ = H // Q
+FLOPS = 2 * B * S * D * KVL + 2 * B * S * KVL * H * 256
+
+
+def tile_ssa_pb_kernel(tc, x, wkv_c, wkv_b, out_0, out_1):
+    nc = tc.nc
+    with ExitStack() as ctx:
+        const = ctx.enter_context(tc.tile_pool(name="const", bufs=1))
+        inputs = ctx.enter_context(tc.tile_pool(name="inputs", bufs=8))
+        stage = ctx.enter_context(tc.tile_pool(name="stage", bufs=3))
+        keep = ctx.enter_context(tc.tile_pool(name="keep", bufs=1))
+        outs = ctx.enter_context(tc.tile_pool(name="outs", bufs=3))
+        small = ctx.enter_context(tc.tile_pool(name="small", bufs=2))
+        psum = ctx.enter_context(tc.psum_pool(name="psum", bufs=8))
+        ctx.enter_context(tc.manual_schedule())
+
+        x_view = x.rearrange("b (p r) d -> b p r d", r=2)
+        wc_view = wkv_c.rearrange("(p e) d -> p e d", e=4)
+        wb_view = wkv_b.rearrange("(i h c e) k -> i c h (e k)", i=NQ, h=Q, e=2)
+        k_view = out_0.rearrange("b (p r) h d -> b p r (h d)", r=2)
+        v_view = out_1.rearrange("b (p r) h d -> b p r (h d)", r=2)
+
+        wc_raw, x_raw, wb_raw = [], [], []
+        for kh in range(2):
+            t = inputs.tile([P, 4, D // 2], BF16, name="wc_raw%d" % kh, tag="in")
+            wc_raw.append(t)
+            k0 = D // 2 * kh
+            if kh == 0:
+                for g in range(2):
+                    nc.sync.dma_start(out=t[:, :, 512 * g : 512 * g + 512], in_=wc_view[:, :, 512 * g : 512 * g + 512])
+            else:
+                nc.sync.dma_start(out=t[:], in_=wc_view[:, :, k0 : k0 + D // 2])
+
+        def load_x(b):
+            t = inputs.tile([P, 2, D], BF16, name="x_raw%d" % b, tag="in")
+            x_raw.append(t)
+            if b == 0:
+                for r in range(2):
+                    nc.sync.dma_start(out=t[:, r, :], in_=x_view[b, :, r, :])
+            else:
+                nc.sync.dma_start(out=t[:], in_=x_view[b])
+
+        load_x(0)
+        for i in range(NQ):
+            t = inputs.tile([P, Q, 2 * KVL], BF16, name="wb_raw%d" % i, tag="in")
+            nc.sync.dma_start(out=t[:], in_=wb_view[i])
+            wb_raw.append(t)
+        load_x(1)
+
+        ident = const.tile([P, P], F32, name="ident")
+        make_identity(nc, ident[:])
+        warm = const.tile([P, 2], F32, name="warm")
+        nc.vector.memset(warm[:], 0.0)
+        nc.scalar.activation(out=warm[:, 1:2], in_=warm[:, 0:1], func=ACT.Silu)
+
+        wc_codes = keep.tile([P, G, KVL], U32, name="wc_codes", align_bytes=64)
+        wc_scales = keep.tile([P, G, KVL], U8, name="wc_scales", align_bytes=64)
+        wb_codes = keep.tile([P, NQ, 2, Q * P], U32, name="wb_codes", align_bytes=64)
+        wb_scales = keep.tile([P, NQ, 2, Q * P], U8, name="wb_scales", align_bytes=64)
+
+        live = {}
+
+        def bank(shape):
+            return psum.tile(shape, F32, name="bank", tag="bank")
+
+        def evac(engine, out, in_):
+            if engine == "v":
+                nc.vector.tensor_copy(out=out, in_=in_)
+            else:
+                nc.scalar.copy(out=out, in_=in_)
+
+        def flip4(sources):
+            t = bank([P, 4, P])
+            for i, ap in enumerate(sources):
+                for u in range(2):
+                    words = ap.bitcast(F32)[:, u : u + 2 * P - 1 : 2]
+                    nc.tensor.transpose(t[:, 2 * i + u, :], words, ident[:])
+            return t
+
+        def flip_wc(g, half, engine):
+            if half == 0:
+                live["wc", g] = stage.tile([P, 4 * KVL], BF16, name="wc_stage%d" % g, tag="stage", align_bytes=64)
+            raw = wc_raw[g // 2]
+            k0 = 512 * (g % 2)
+            t = flip4([raw[:, 2 * half + e, k0 : k0 + 512] for e in range(2)])
+            dst = live["wc", g][:].bitcast(F32).rearrange("q (e c u) -> q e c u", e=4, u=2)
+            evac(engine, dst[:, 2 * half : 2 * half + 2], t[:].rearrange("q (e u) c -> q e c u", u=2))
+
+        def quantise_wc(g):
+            nc.vector.quantize_mx(
+                out=wc_codes[:, g, :].bitcast(FP8X4), scales=wc_scales[:, g, :], in_=live["wc", g][:]
+            )
+
+        def flip_x(b, r, half, engine):
+            if half == 0:
+                live["x", b, r] = stage.tile([P, 4 * KVL], BF16, name="x_stage%d%d" % (b, r), tag="stage", align_bytes=64)
+            t = flip4([x_raw[b][:, r, 512 * g : 512 * g + 512] for g in (2 * half, 2 * half + 1)])
+            dst = live["x", b, r][:].bitcast(F32).rearrange("q (g c u) -> q g c u", g=G, u=2)
+            evac(engine, dst[:, 2 * half : 2 * half + 2], t[:].rearrange("q (g u) c -> q g c u", u=2))
+
+        def quantise_x(b, r):
+            codes = small.tile([P, G, P], U32, name="x_codes%d%d" % (b, r), tag="x_codes", bufs=4, align_bytes=64)
+            scales = small.tile([P, G, P], U8, name="x_scales%d%d" % (b, r), tag="x_scales", bufs=4, align_bytes=64)
+            live["xq", b, r] = codes, scales
+            nc.vector.quantize_mx(
+                out=codes[:].rearrange("p g c -> p (g c)").bitcast(FP8X4),
+                scales=scales[:].rearrange("p g c -> p (g c)"),
+                in_=live["x", b, r][:],
+            )
+
+        def flip_wb(i, h, engine):
+            if h == 0:
+                live["wb", i] = stage.tile([P, 2, Q * P * 4], BF16, name="wb_stage%d" % i, tag="wb_stage", bufs=2, align_bytes=64)
+            t = flip4([wb_raw[i][:, h, KVL * e : KVL * e + KVL] for e in range(2)])
+            dst = live["wb", i][:].rearrange("q v n -> q (v n)").bitcast(F32).rearrange(
+                "q (v h c a) -> q v h c a", v=2, h=Q, a=4
+            )
+            evac(engine, dst[:, :, h], t[:].rearrange("q a (v c) -> q v c a", v=2))
+
+        def quantise_wb(i, v):
+            nc.vector.quantize_mx(
+                out=wb_codes[:, i, v, :].bitcast(FP8X4), scales=wb_scales[:, i, v, :], in_=live["wb", i][:, v, :]
+            )
+
+        def stage1(b, r):
+            acc = bank([P, 4, P])
+            live["m1", b, r] = acc
+            codes, scales = live["xq", b, r]
+            for j in range(4):
+                rows = slice(P * j, P * j + P)
+                for g in range(G):
+                    nc.tensor.matmul_mx(
+                        out=acc[:, j, :],
+                        lhsT=wc_codes[:, g, rows].bitcast(FP8X4),
+                        lhsT_scale=wc_scales[:, g, rows],
+                        rhs=codes[:, g, :].bitcast(FP8X4),
+                        rhs_scale=scales[:, g, :],
+                        start=(g == 0),
+                        stop=(g == G - 1),
+                    )
+
+        def stage1_out(b, r, engine):
+            kv = stage.tile([P, P, 4], BF16, name="kv%d%d" % (b, r), tag="kv", align_bytes=64)
+            live["kv", b, r] = kv
+            evac(engine, kv[:], live["m1", b, r][:].rearrange("q j t -> q t j"))
+
+        def stage1_quantise(b, r):
+            codes = small.tile([P, P], U32, name="kv_codes%d%d" % (b, r), tag="kv_codes", bufs=4, align_bytes=64)
+            scales = small.tile([P, P], U8, name="kv_scales%d%d" % (b, r), tag="kv_scales", bufs=4, align_bytes=64)
+            live["kvq", b, r] = codes, scales
+            nc.vector.quantize_mx(
+                out=codes[:].bitcast(FP8X4), scales=scales[:], in_=live["kv", b, r][:].rearrange("q t j -> q (t j)")
+            )
+
+        def product(b, r, v, i, engine):
+            t = bank([P, 512])
+            codes, scales = live["kvq", b, r]
+            nc.tensor.matmul_mx(
+                out=t[:],
+                lhsT=codes[:].bitcast(FP8X4),
+                lhsT_scale=scales[:],
+                rhs=wb_codes[:, i, v, :].bitcast(FP8X4),
+                rhs_scale=wb_scales[:, i, v, :],
+                start=True,
+                stop=True,
+            )
+            if ("out", b, v) not in live:
+                live["out", b, v] = outs.tile([P, 2, H * P], F32, name="out%d%d" % (b, v), tag="out%d" % v)
+            dst = live["out", b, v][:, r, 512 * i : 512 * i + 512]
+            if v == 0:
+                nc.scalar.activation(out=dst, in_=t[:], func=ACT.Silu)
+            else:
+                evac(engine, dst, t[:])
+
+        def part_max(b, i0, n):
+            if ("pm", b) not in live:
+                live["pm", b] = [small.tile([P, NQ], F32, name="pm%d" % b, tag="pm"), 0]
+            pm, j = live["pm", b]
+            nc.vector.tensor_reduce(
+                out=pm[:, j : j + 1],
+                in_=live["out", b, 0][:, :, 512 * i0 : 512 * (i0 + n)],
+                axis=AX.XY,
+                op=ALU.max,
+            )
+            live["pm", b][1] = j + 1
+
+        def flip_max(b):
+            pm, n = live["pm", b]
+            t = bank([P, 4, P])
+            live["ft", b] = t
+            for j in range(n):
+                nc.tensor.transpose(t[:, j, :], pm[:, j : j + 1].to_broadcast([P, P]), ident[:])
+
+        def factors(b):
+            n = live["pm", b][1]
+            m = small.tile([P, H], F32, name="m%d" % b, tag="m")
+            nc.vector.tensor_reduce(
+                out=m[:],
+                in_=live["ft", b][:, 0:n, :].rearrange("q j (g s) -> q g j s", s=8),
+                axis=AX.XY,
+                op=ALU.max,
+            )
+            z = small.tile([P, H], F32, name="z%d" % b, tag="z")
+            nc.vector.scalar_tensor_tensor(
+                out=z[:], in0=m[:], scalar=0.0, in1=m[:], op0=ALU.is_equal, op1=ALU.add
+            )
+            rc = small.tile([P, H], F32, name="rc%d" % b, tag="rc")
+            nc.vector.reciprocal(out=rc[:], in_=z[:])
+            eta = small.tile([P, H], F32, name="eta%d" % b, tag="eta")
+            nc.vector.tensor_scalar(
+                out=eta[:], in0=rc[:], scalar1=10.0, scalar2=1.0, op0=ALU.mult, op1=ALU.min
+            )
+            live["eta", b] = eta
+
+        def scale_head(b, h, engine):
+            a = live["out", b, 0][:, :, P * h : P * h + P]
+            eta = live["eta", b][:, h : h + 1]
+            if engine == "g":
+                nc.gpsimd.tensor_scalar(out=a, in0=a, scalar1=eta, scalar2=1.0, op0=ALU.mult, op1=ALU.mult)
+            elif engine == "v":
+                nc.vector.tensor_scalar(out=a, in0=a, scalar1=eta, scalar2=None, op0=ALU.mult)
+            else:
+                nc.scalar.activation(out=a, in_=a, func=ACT.Copy, scale=eta)
+
+        def store(b, v, i0, n):
+            view = (k_view, v_view)[v]
+            cols = slice(512 * i0, 512 * (i0 + n))
+            nc.sync.dma_start(out=view[b, :, :, cols], in_=live["out", b, v][:, :, cols])
+
+
+        pending = []
+
+        def later(lag, step):
+            pending.append([lag, step])
+
+        def tick():
+            for entry in pending:
+                entry[0] -= 1
+            for entry in [e for e in pending if e[0] <= 0]:
+                pending.remove(entry)
+                entry[1]()
+
+        def do_wc(g, half, engine):
+            flip_wc(g, half, engine)
+            if half == 1:
+                later(2, lambda: quantise_wc(g))
+            tick()
+
+        def do_x(b, r):
+            for half in range(2):
+                flip_x(b, r, half, "ss"[half])
+                if half == 1:
+                    later(2, lambda: quantise_x(b, r))
+                tick()
+
+        def do_wb(i, h, engine):
+            flip_wb(i, h, engine)
+            if h == Q - 1:
+                later(2, lambda: quantise_wb(i, 0))
+                later(3, lambda: quantise_wb(i, 1))
+            tick()
+
+        def do_stage1(b, r):
+            stage1(b, r)
+            stage1_out(b, r, "ss"[r])
+            later(1, lambda: stage1_quantise(b, r))
+            tick()
+
+        def do_product(b, r, v, i, engine):
+            product(b, r, v, i, engine)
+            if r == 1:
+                if v == 0:
+                    later(1, lambda: part_max(b, i, 1))
+                else:
+                    later(1, lambda: store(b, 1, i, 1))
+            tick()
+
+        def finish_keys(b, engines):
+            fl = [3,7,7,4][b]
+            later(fl, lambda: flip_max(b))
+            later(fl + 1, lambda: factors(b))
+            for h in range(H):
+                later(fl + 2, lambda h=h: scale_head(b, h, engines[h % len(engines)]))
+                if b + 1 < B:
+                    if h % 8 == 7:
+                        later(fl + 2 + [8,14][h // 8], lambda h=h: store(b, 0, (h - 7) // Q, 2))
+                elif h % 4 == 3:
+                    later(fl + 2, lambda h=h: store(b, 0, h // Q, 1))
+
+        def do_quad(b, i):
+            for r in range(2):
+                do_product(b, r, 1, i, ["vv","vs"][i % 2][r])
+                do_product(b, r, 0, i, "s")
+
+        for g in range(G):
+            do_wc(g, 0, "s")
+            do_wc(g, 1, "v")
+        for r in range(2):
+            do_x(0, r)
+        do_wb(0, 0, "svss"[0])
+        do_wb(0, 1, "svss"[1])
+        do_stage1(0, 0)
+        do_wb(0, 2, "svss"[2])
+        do_wb(0, 3, "svss"[3])
+        do_stage1(0, 1)
+        for i in range(NQ):
+            if i + 1 < NQ:
+                for h in range(Q):
+                    do_wb(i + 1, h, "svss"[h])
+            else:
+                do_x(1, 0)
+                do_x(1, 1)
+            if i in (0, 1):
+                load_x(2 + i)
+            do_quad(0, i)
+            if i == NQ - 2:
+                pass
+        finish_keys(0, ["g", "g", "g"][0])
+        do_stage1(1, 0)
+        do_stage1(1, 1)
+        for b in range(1, B):
+            if b + 1 < B:
+                for i in range(NQ):
+                    if i < 2:
+                        do_x(b + 1, i)
+                    else:
+                        do_stage1(b + 1, i - 2)
+                    do_quad(b, i)
+                finish_keys(b, ["g", "g", "g"][b])
+            else:
+                for i in range(NQ):
+                    for r in range(2):
+                        do_product(b, r, 0, i, "s")
+                    if i:
+                        do_product(b, 0, 1, i - 1, "v")
+                finish_keys(b, "vvs")
+                for i in range(NQ):
+                    if i == NQ - 1:
+                        do_product(b, 0, 1, i, "v")
+                    do_product(b, 1, 1, i, "s")
+        while pending:
+            tick()

@@ -39,15 +39,6 @@ def tile_ssa_pb_kernel(tc, x, wkv_c, wkv_b, out_0, out_1):
         v_view = out_1.rearrange("b (p r) h d -> b p r (h d)", r=2)
 
         wc_raw, x_raw, wb_raw = [], [], []
-        for kh in range(2):
-            t = inputs.tile([P, 4, D // 2], BF16, name="wc_raw%d" % kh, tag="in")
-            wc_raw.append(t)
-            k0 = D // 2 * kh
-            if kh == 0:
-                for g in range(2):
-                    nc.sync.dma_start(out=t[:, :, 512 * g : 512 * g + 512], in_=wc_view[:, :, 512 * g : 512 * g + 512])
-            else:
-                nc.sync.dma_start(out=t[:], in_=wc_view[:, :, k0 : k0 + D // 2])
 
         def load_x(b):
             t = inputs.tile([P, 2, D], BF16, name="x_raw%d" % b, tag="in")
@@ -59,6 +50,10 @@ def tile_ssa_pb_kernel(tc, x, wkv_c, wkv_b, out_0, out_1):
                 nc.sync.dma_start(out=t[:], in_=x_view[b])
 
         load_x(0)
+        for half in range(2):
+            t = inputs.tile([P, 2, D], BF16, name="wc_raw%d" % half, tag="in")
+            nc.sync.dma_start(out=t[:], in_=wc_view[:, 2 * half : 2 * half + 2, :])
+            wc_raw.append(t)
         for i in range(NQ):
             t = inputs.tile([P, Q, 2 * KVL], BF16, name="wb_raw%d" % i, tag="in")
             nc.sync.dma_start(out=t[:], in_=wb_view[i])
@@ -97,10 +92,8 @@ def tile_ssa_pb_kernel(tc, x, wkv_c, wkv_b, out_0, out_1):
 
         def flip_wc(g, half, engine):
             if half == 0:
-                live["wc", g] = stage.tile([P, 4 * KVL], BF16, name="wc_stage%d" % g, tag="stage", align_bytes=64)
-            raw = wc_raw[g // 2]
-            k0 = 512 * (g % 2)
-            t = flip4([raw[:, 2 * half + e, k0 : k0 + 512] for e in range(2)])
+                live["wc", g] = stage.tile([P, 4 * KVL], BF16, name="wc_stage%d" % g, tag="stage", bufs=6, align_bytes=64)
+            t = flip4([wc_raw[half][:, e, 512 * g : 512 * g + 512] for e in range(2)])
             dst = live["wc", g][:].bitcast(F32).rearrange("q (e c u) -> q e c u", e=4, u=2)
             evac(engine, dst[:, 2 * half : 2 * half + 2], t[:].rearrange("q (e u) c -> q e c u", u=2))
 
@@ -111,7 +104,7 @@ def tile_ssa_pb_kernel(tc, x, wkv_c, wkv_b, out_0, out_1):
 
         def flip_x(b, r, half, engine):
             if half == 0:
-                live["x", b, r] = stage.tile([P, 4 * KVL], BF16, name="x_stage%d%d" % (b, r), tag="stage", align_bytes=64)
+                live["x", b, r] = stage.tile([P, 4 * KVL], BF16, name="x_stage%d%d" % (b, r), tag="stage", bufs=6, align_bytes=64)
             t = flip4([x_raw[b][:, r, 512 * g : 512 * g + 512] for g in (2 * half, 2 * half + 1)])
             dst = live["x", b, r][:].bitcast(F32).rearrange("q (g c u) -> q g c u", g=G, u=2)
             evac(engine, dst[:, 2 * half : 2 * half + 2], t[:].rearrange("q (g u) c -> q g c u", u=2))
@@ -183,7 +176,7 @@ def tile_ssa_pb_kernel(tc, x, wkv_c, wkv_b, out_0, out_1):
                 stop=True,
             )
             if ("out", b, v) not in live:
-                live["out", b, v] = outs.tile([P, 2, H * P], F32, name="out%d%d" % (b, v), tag="out%d" % v)
+                live["out", b, v] = outs.tile([P, 2, H * P], F32, name="out%d%d" % (b, v), tag="out%d" % v, bufs=3 - v)
             dst = live["out", b, v][:, r, 512 * i : 512 * i + 512]
             if v == 0:
                 nc.scalar.activation(out=dst, in_=t[:], func=ACT.Silu)
@@ -258,6 +251,11 @@ def tile_ssa_pb_kernel(tc, x, wkv_c, wkv_b, out_0, out_1):
                 pending.remove(entry)
                 entry[1]()
 
+        def tick0():
+            for entry in [e for e in pending if e[0] <= 0]:
+                pending.remove(entry)
+                entry[1]()
+
         def do_wc(g, half, engine):
             flip_wc(g, half, engine)
             if half == 1:
@@ -266,9 +264,9 @@ def tile_ssa_pb_kernel(tc, x, wkv_c, wkv_b, out_0, out_1):
 
         def do_x(b, r):
             for half in range(2):
-                flip_x(b, r, half, "ss"[half])
+                flip_x(b, r, half, ("svss" if b else "svsv")[2 * r + half])
                 if half == 1:
-                    later(2, lambda: quantise_x(b, r))
+                    later(1, lambda: quantise_x(b, r))
                 tick()
 
         def do_wb(i, h, engine):
@@ -280,81 +278,80 @@ def tile_ssa_pb_kernel(tc, x, wkv_c, wkv_b, out_0, out_1):
 
         def do_stage1(b, r):
             stage1(b, r)
-            stage1_out(b, r, "ss"[r])
+            stage1_out(b, r, "sv"[r])
             later(1, lambda: stage1_quantise(b, r))
             tick()
 
-        def do_product(b, r, v, i, engine):
-            product(b, r, v, i, engine)
-            if r == 1:
-                if v == 0:
-                    later(1, lambda: part_max(b, i, 1))
-                else:
-                    later(1, lambda: store(b, 1, i, 1))
-            tick()
-
-        def finish_keys(b, engines):
-            fl = [3,7,7,4][b]
-            later(fl, lambda: flip_max(b))
-            later(fl + 1, lambda: factors(b))
-            for h in range(H):
-                later(fl + 2, lambda h=h: scale_head(b, h, engines[h % len(engines)]))
-                if b + 1 < B:
-                    if h % 8 == 7:
-                        later(fl + 2 + [8,14][h // 8], lambda h=h: store(b, 0, (h - 7) // Q, 2))
-                elif h % 4 == 3:
-                    later(fl + 2, lambda h=h: store(b, 0, h // Q, 1))
-
-        def do_quad(b, i):
+        def do_keys(b, i):
             for r in range(2):
-                do_product(b, r, 1, i, ["vv","vs"][i % 2][r])
-                do_product(b, r, 0, i, "s")
+                product(b, r, 0, i, "s")
+                if r == 1:
+                    later(1, lambda: part_max(b, i, 1))
+                tick()
 
-        for g in range(G):
-            do_wc(g, 0, "s")
-            do_wc(g, 1, "v")
+        def do_values(b, i, engines):
+            for r in range(2):
+                product(b, r, 1, i, engines[r])
+                if r == 1 and i % 1 == 1 - 1:
+                    later(1, lambda: store(b, 1, i + 1 - 1, 1))
+                tick()
+
+        def finish_keys(b):
+            step = [0.5,0.5,0.5,0][b]
+            klag = [[1,1],[1,1],[1,1],[0,0]][b]
+            engines = ["v","v","v","vvs"][b]
+            start = [1,1,1,0][b]
+            flip_max(b)
+            later([0,0,0,0][b], lambda: factors(b))
+            for h in range(H):
+                later(start + int(h * step), lambda h=h: scale_head(b, h, engines[h % len(engines)]))
+                if b + 1 < B:
+                    if h % (4 * 2) == 4 * 2 - 1:
+                        later(start + int(h * step) + klag[h // 8], lambda h=h: store(b, 0, h // Q + 1 - 2, 2))
+                elif h % 4 == 3:
+                    later(start + int(h * step), lambda h=h: store(b, 0, h // Q, 1))
+            if [0,0,0,0][b] == 0:
+                tick0()
+
         for r in range(2):
             do_x(0, r)
+        for half in range(2):
+            for g in range(G):
+                do_wc(g, half, "sv"[g % 2])
         do_wb(0, 0, "svss"[0])
         do_wb(0, 1, "svss"[1])
-        do_stage1(0, 0)
         do_wb(0, 2, "svss"[2])
         do_wb(0, 3, "svss"[3])
+        do_stage1(0, 0)
         do_stage1(0, 1)
-        for i in range(NQ):
-            if i + 1 < NQ:
-                for h in range(Q):
-                    do_wb(i + 1, h, "svss"[h])
-            else:
-                do_x(1, 0)
-                do_x(1, 1)
-            if i in (0, 1):
-                load_x(2 + i)
-            do_quad(0, i)
-            if i == NQ - 2:
-                pass
-        finish_keys(0, ["g", "g", "g"][0])
-        do_stage1(1, 0)
-        do_stage1(1, 1)
-        for b in range(1, B):
-            if b + 1 < B:
-                for i in range(NQ):
-                    if i < 2:
-                        do_x(b + 1, i)
-                    else:
-                        do_stage1(b + 1, i - 2)
-                    do_quad(b, i)
-                finish_keys(b, ["g", "g", "g"][b])
-            else:
-                for i in range(NQ):
-                    for r in range(2):
-                        do_product(b, r, 0, i, "s")
-                    if i:
-                        do_product(b, 0, 1, i - 1, "v")
-                finish_keys(b, "vvs")
-                for i in range(NQ):
-                    if i == NQ - 1:
-                        do_product(b, 0, 1, i, "v")
-                    do_product(b, 1, 1, i, "s")
+        patterns = ["WLWLWKKKKXVXVFMVMVXX","KKMKKMVXVFXVV","KKMKKMVVFVV","KKKKVVVFV"]
+        nv = 0
+        ahead = dict(X=0, M=0)
+        for b in range(B):
+            count = dict(L=0, W=0, K=0, V=0)
+            for step in patterns[b]:
+                n = ahead[step] if step in "XM" else count.get(step)
+                if step == "W":
+                    for h in range(Q):
+                        do_wb(n + 1, h, "svss"[h])
+                elif step == "K":
+                    do_keys(b, n)
+                elif step == "V":
+                    do_values(b, n, ["ssssssss","ssssssss","ssssssss","ssssssvs"][b][2 * n : 2 * n + 2])
+                    nv += 1
+                    if nv in []:
+                        load_x(len(x_raw))
+                elif step == "L":
+                    load_x(len(x_raw))
+                elif step == "X":
+                    do_x(1 + n // 2, n % 2)
+                elif step == "M":
+                    do_stage1(1 + n // 2, n % 2)
+                else:
+                    finish_keys(b)
+                if step in "XM":
+                    ahead[step] += 1
+                elif step != "F":
+                    count[step] += 1
         while pending:
             tick()

@@ -34,7 +34,7 @@ def tile_ssa_pb_kernel(tc, x, wkv_c, wkv_b, out_0, out_1):
 
         x_view = x.rearrange("b (p r) d -> b p r d", r=2)
         wc_view = wkv_c.rearrange("(p e) d -> p e d", e=4)
-        wb_view = wkv_b.rearrange("(i h c e) k -> i c h (e k)", i=NQ, h=Q, e=2)
+        wb_view = wkv_b.rearrange("(i c e) k -> i c e k", i=NQ, e=8)
         k_view = out_0.rearrange("b (p r) h d -> b p r (h d)", r=2)
         v_view = out_1.rearrange("b (p r) h d -> b p r (h d)", r=2)
 
@@ -55,7 +55,7 @@ def tile_ssa_pb_kernel(tc, x, wkv_c, wkv_b, out_0, out_1):
             nc.sync.dma_start(out=t[:], in_=wc_view[:, 2 * half : 2 * half + 2, :])
             wc_raw.append(t)
         for i in range(NQ):
-            t = inputs.tile([P, Q, 2 * KVL], BF16, name="wb_raw%d" % i, tag="in")
+            t = inputs.tile([P, 8, KVL], BF16, name="wb_raw%d" % i, tag="in")
             nc.sync.dma_start(out=t[:], in_=wb_view[i])
             wb_raw.append(t)
         load_x(1)
@@ -119,19 +119,21 @@ def tile_ssa_pb_kernel(tc, x, wkv_c, wkv_b, out_0, out_1):
                 in_=live["x", b, r][:],
             )
 
-        def flip_wb(i, h, engine):
-            if h == 0:
-                live["wb", i] = stage.tile([P, 2, Q * P * 4], BF16, name="wb_stage%d" % i, tag="wb_stage", bufs=2, align_bytes=64)
-            t = flip4([wb_raw[i][:, h, KVL * e : KVL * e + KVL] for e in range(2)])
-            dst = live["wb", i][:].rearrange("q v n -> q (v n)").bitcast(F32).rearrange(
-                "q (v h c a) -> q v h c a", v=2, h=Q, a=4
-            )
-            evac(engine, dst[:, :, h], t[:].rearrange("q a (v c) -> q v c a", v=2))
+        def flip_wb(i, n, engine):
+            if n == 0:
+                live["wb", i] = stage.tile([P, 2 * Q, P * 4], BF16, name="wb_stage%d" % i, tag="wb_stage", bufs=2, align_bytes=64)
+            t = flip4([wb_raw[i][:, 2 * n + e, :] for e in range(2)])
+            dst = live["wb", i][:].rearrange("q m n -> q (m n)").bitcast(F32).rearrange("q (c n a) -> q c n a", c=P, a=4)
+            evac(engine, dst[:, :, n], t[:].rearrange("q a c -> q c a"))
 
         def quantise_wb(i, v):
-            nc.vector.quantize_mx(
-                out=wb_codes[:, i, v, :].bitcast(FP8X4), scales=wb_scales[:, i, v, :], in_=live["wb", i][:, v, :]
-            )
+            for h in range(Q):
+                cols = slice(P * h, P * h + P)
+                nc.vector.quantize_mx(
+                    out=wb_codes[:, i, v, cols].bitcast(FP8X4),
+                    scales=wb_scales[:, i, v, cols],
+                    in_=live["wb", i][:, 2 * h + v, :],
+                )
 
         def stage1(b, r):
             acc = bank([P, 4, P])
@@ -183,33 +185,30 @@ def tile_ssa_pb_kernel(tc, x, wkv_c, wkv_b, out_0, out_1):
             else:
                 evac(engine, dst, t[:])
 
-        def part_max(b, i0, n):
+        def part_max(b, r, half):
             if ("pm", b) not in live:
-                live["pm", b] = [small.tile([P, NQ], F32, name="pm%d" % b, tag="pm"), 0]
-            pm, j = live["pm", b]
+                live["pm", b] = small.tile([P, 4], F32, name="pm%d" % b, tag="pm")
             nc.vector.tensor_reduce(
-                out=pm[:, j : j + 1],
-                in_=live["out", b, 0][:, :, 512 * i0 : 512 * (i0 + n)],
-                axis=AX.XY,
+                out=live["pm", b][:, 2 * r + half : 2 * r + half + 1],
+                in_=live["out", b, 0][:, r, 1024 * half : 1024 * half + 1024],
+                axis=AX.X,
                 op=ALU.max,
             )
-            live["pm", b][1] = j + 1
+
+        def whole_max(b):
+            tm = small.tile([P, 1], F32, name="tm%d" % b, tag="tm")
+            nc.vector.tensor_reduce(out=tm[:], in_=live["pm", b][:], axis=AX.X, op=ALU.max)
+            live["tm", b] = tm
 
         def flip_max(b):
-            pm, n = live["pm", b]
             t = bank([P, 4, P])
             live["ft", b] = t
-            for j in range(n):
-                nc.tensor.transpose(t[:, j, :], pm[:, j : j + 1].to_broadcast([P, P]), ident[:])
+            nc.tensor.transpose(t[:, 0, :], live["tm", b][:].to_broadcast([P, P]), ident[:])
 
         def factors(b):
-            n = live["pm", b][1]
             m = small.tile([P, H], F32, name="m%d" % b, tag="m")
             nc.vector.tensor_reduce(
-                out=m[:],
-                in_=live["ft", b][:, 0:n, :].rearrange("q j (g s) -> q g j s", s=8),
-                axis=AX.XY,
-                op=ALU.max,
+                out=m[:], in_=live["ft", b][:, 0, :].rearrange("q (g s) -> q g s", s=8), axis=AX.X, op=ALU.max
             )
             z = small.tile([P, H], F32, name="z%d" % b, tag="z")
             nc.vector.scalar_tensor_tensor(
@@ -233,10 +232,13 @@ def tile_ssa_pb_kernel(tc, x, wkv_c, wkv_b, out_0, out_1):
             else:
                 nc.scalar.activation(out=a, in_=a, func=ACT.Copy, scale=eta)
 
-        def store(b, v, i0, n):
-            view = (k_view, v_view)[v]
+        def store_values(b, r, i0, n):
             cols = slice(512 * i0, 512 * (i0 + n))
-            nc.sync.dma_start(out=view[b, :, :, cols], in_=live["out", b, v][:, :, cols])
+            nc.sync.dma_start(out=v_view[b, :, r, cols], in_=live["out", b, 1][:, r, cols])
+
+        def store_keys(b, i0, n):
+            cols = slice(512 * i0, 512 * (i0 + n))
+            nc.sync.dma_start(out=k_view[b, :, :, cols], in_=live["out", b, 0][:, :, cols])
 
 
         pending = []
@@ -244,17 +246,15 @@ def tile_ssa_pb_kernel(tc, x, wkv_c, wkv_b, out_0, out_1):
         def later(lag, step):
             pending.append([lag, step])
 
-        def tick():
-            for entry in pending:
-                entry[0] -= 1
+        def flush():
             for entry in [e for e in pending if e[0] <= 0]:
                 pending.remove(entry)
                 entry[1]()
 
-        def tick0():
-            for entry in [e for e in pending if e[0] <= 0]:
-                pending.remove(entry)
-                entry[1]()
+        def tick():
+            for entry in pending:
+                entry[0] -= 1
+            flush()
 
         def do_wc(g, half, engine):
             flip_wc(g, half, engine)
@@ -269,12 +269,13 @@ def tile_ssa_pb_kernel(tc, x, wkv_c, wkv_b, out_0, out_1):
                     later(1, lambda: quantise_x(b, r))
                 tick()
 
-        def do_wb(i, h, engine):
-            flip_wb(i, h, engine)
-            if h == Q - 1:
-                later(2, lambda: quantise_wb(i, 0))
-                later(3, lambda: quantise_wb(i, 1))
-            tick()
+        def do_wb(i):
+            for n in range(4):
+                flip_wb(i, n, "svss"[n])
+                if n == 3:
+                    later(2, lambda: quantise_wb(i, 0))
+                    later(3, lambda: quantise_wb(i, 1))
+                tick()
 
         def do_stage1(b, r):
             stage1(b, r)
@@ -282,18 +283,22 @@ def tile_ssa_pb_kernel(tc, x, wkv_c, wkv_b, out_0, out_1):
             later(1, lambda: stage1_quantise(b, r))
             tick()
 
-        def do_keys(b, i):
-            for r in range(2):
+        def do_keys(b, r, half):
+            for i in (2 * half, 2 * half + 1):
                 product(b, r, 0, i, "s")
-                if r == 1:
-                    later(1, lambda: part_max(b, i, 1))
+                if i == 2 * half + 1:
+                    later(1, lambda: part_max(b, r, half))
+                    if r == 1 and half == 1:
+                        later(1, lambda: whole_max(b))
                 tick()
 
-        def do_values(b, i, engines):
-            for r in range(2):
-                product(b, r, 1, i, engines[r])
-                if r == 1 and i % 1 == 1 - 1:
-                    later(1, lambda: store(b, 1, i + 1 - 1, 1))
+        def do_values(b, r, half):
+            for i in (2 * half, 2 * half + 1):
+                product(b, r, 1, i, ["ssssssss","ssssssss","ssssssss","ssssssvs"][b][4 * r + i])
+                if 2 == 4 and i == 3:
+                    later(1, lambda: store_values(b, r, 0, 4))
+                elif 2 == 2 and i == 2 * half + 1:
+                    later(1, lambda: store_values(b, r, 2 * half, 2))
                 tick()
 
         def finish_keys(b):
@@ -302,54 +307,41 @@ def tile_ssa_pb_kernel(tc, x, wkv_c, wkv_b, out_0, out_1):
             engines = ["v","v","v","vvs"][b]
             start = [1,1,1,0][b]
             flip_max(b)
-            later([0,0,0,0][b], lambda: factors(b))
+            later(0, lambda: factors(b))
             for h in range(H):
                 later(start + int(h * step), lambda h=h: scale_head(b, h, engines[h % len(engines)]))
                 if b + 1 < B:
                     if h % (4 * 2) == 4 * 2 - 1:
-                        later(start + int(h * step) + klag[h // 8], lambda h=h: store(b, 0, h // Q + 1 - 2, 2))
+                        later(start + int(h * step) + klag[h // 8], lambda h=h: store_keys(b, h // Q + 1 - 2, 2))
                 elif h % 4 == 3:
-                    later(start + int(h * step), lambda h=h: store(b, 0, h // Q, 1))
-            if [0,0,0,0][b] == 0:
-                tick0()
+                    later(start + int(h * step), lambda h=h: store_keys(b, h // Q, 1))
+            flush()
 
-        for r in range(2):
-            do_x(0, r)
-        for half in range(2):
-            for g in range(G):
-                do_wc(g, half, "sv"[g % 2])
-        do_wb(0, 0, "svss"[0])
-        do_wb(0, 1, "svss"[1])
-        do_wb(0, 2, "svss"[2])
-        do_wb(0, 3, "svss"[3])
-        do_stage1(0, 0)
-        do_stage1(0, 1)
-        patterns = ["WLWLWKKKKXVXVFMVMVXX","KKMKKMVXVFXVV","KKMKKMVVFVV","KKKKVVVFV"]
-        nv = 0
-        ahead = dict(X=0, M=0)
+        patterns = ["xxwwwwwwwwWMMWLWLWKKKKXXVVFVMMVX","KKKKVXVVFMVMX","KKKKVXVVFMVM","KKKKVVVFV"]
+        ahead = dict(X=0, M=0, W=0, x=0, w=0)
         for b in range(B):
-            count = dict(L=0, W=0, K=0, V=0)
+            count = dict(L=0, K=0, V=0)
             for step in patterns[b]:
-                n = ahead[step] if step in "XM" else count.get(step)
-                if step == "W":
-                    for h in range(Q):
-                        do_wb(n + 1, h, "svss"[h])
+                n = ahead[step] if step in ahead else count.get(step)
+                if step == "x":
+                    do_x(0, n)
+                elif step == "w":
+                    do_wc(n % G, n // G, "sv"[n % 2])
+                elif step == "W":
+                    do_wb(n)
                 elif step == "K":
-                    do_keys(b, n)
+                    do_keys(b, n // 2, n % 2)
                 elif step == "V":
-                    do_values(b, n, ["ssssssss","ssssssss","ssssssss","ssssssvs"][b][2 * n : 2 * n + 2])
-                    nv += 1
-                    if nv in []:
-                        load_x(len(x_raw))
+                    do_values(b, n // 2, n % 2)
                 elif step == "L":
                     load_x(len(x_raw))
                 elif step == "X":
                     do_x(1 + n // 2, n % 2)
                 elif step == "M":
-                    do_stage1(1 + n // 2, n % 2)
+                    do_stage1(n // 2, n % 2)
                 else:
                     finish_keys(b)
-                if step in "XM":
+                if step in ahead:
                     ahead[step] += 1
                 elif step != "F":
                     count[step] += 1

from contextlib import ExitStack

import concourse.mybir as mybir
from concourse.masks import make_identity

F32 = mybir.dt.float32
BF16 = mybir.dt.bfloat16
U32 = mybir.dt.uint32
U8 = mybir.dt.uint8
FP8X4 = mybir.dt.float8_e4m3fn_x4
ACT = mybir.ActivationFunctionType
ALU = mybir.AluOpType
AX = mybir.AxisListType

P = 128
B, S, D, H, KVL = 4, 256, 2048, 16, 512
G = D // 512
Q = 4
NQ = H // Q
FLOPS = 2 * B * S * D * KVL + 2 * B * S * KVL * H * 256


def tile_ssa_pb_kernel(tc, x, wkv_c, wkv_b, out_0, out_1):
    nc = tc.nc
    with ExitStack() as ctx:
        const = ctx.enter_context(tc.tile_pool(name="const", bufs=1))
        inputs = ctx.enter_context(tc.tile_pool(name="inputs", bufs=8))
        stage = ctx.enter_context(tc.tile_pool(name="stage", bufs=3))
        keep = ctx.enter_context(tc.tile_pool(name="keep", bufs=1))
        outs = ctx.enter_context(tc.tile_pool(name="outs", bufs=3))
        small = ctx.enter_context(tc.tile_pool(name="small", bufs=2))
        psum = ctx.enter_context(tc.psum_pool(name="psum", bufs=8))
        ctx.enter_context(tc.manual_schedule())

        x_view = x.rearrange("b (p r) d -> b p r d", r=2)
        wc_view = wkv_c.rearrange("(p e) d -> p e d", e=4)
        wb_view = wkv_b.rearrange("(i c e) k -> i c e k", i=NQ, e=8)
        k_view = out_0.rearrange("b (p r) h d -> b p r (h d)", r=2)
        v_view = out_1.rearrange("b (p r) h d -> b p r (h d)", r=2)

        wc_raw, x_raw, wb_raw = [], [], []

        def load_x(b):
            t = inputs.tile([P, 2, D], BF16, name="x_raw%d" % b, tag="in")
            x_raw.append(t)
            if b == 0:
                for r in range(2):
                    nc.sync.dma_start(out=t[:, r, :], in_=x_view[b, :, r, :])
            else:
                nc.sync.dma_start(out=t[:], in_=x_view[b])

        load_x(0)
        for half in range(2):
            t = inputs.tile([P, 2, D], BF16, name="wc_raw%d" % half, tag="in")
            nc.sync.dma_start(out=t[:], in_=wc_view[:, 2 * half : 2 * half + 2, :])
            wc_raw.append(t)
        for i in range(NQ):
            t = inputs.tile([P, 8, KVL], BF16, name="wb_raw%d" % i, tag="in")
            nc.sync.dma_start(out=t[:], in_=wb_view[i])
            wb_raw.append(t)
        load_x(1)

        ident = const.tile([P, P], F32, name="ident")
        make_identity(nc, ident[:])
        warm = const.tile([P, 2], F32, name="warm")
        nc.vector.memset(warm[:], 0.0)
        nc.scalar.activation(out=warm[:, 1:2], in_=warm[:, 0:1], func=ACT.Silu)

        wc_codes = keep.tile([P, G, KVL], U32, name="wc_codes", align_bytes=64)
        wc_scales = keep.tile([P, G, KVL], U8, name="wc_scales", align_bytes=64)
        wb_codes = keep.tile([P, NQ, 2, Q * P], U32, name="wb_codes", align_bytes=64)
        wb_scales = keep.tile([P, NQ, 2, Q * P], U8, name="wb_scales", align_bytes=64)

        live = {}

        def bank(shape):
            return psum.tile(shape, F32, name="bank", tag="bank")

        def evac(engine, out, in_):
            if engine == "v":
                nc.vector.tensor_copy(out=out, in_=in_)
            else:
                nc.scalar.copy(out=out, in_=in_)

        def flip4(sources):
            t = bank([P, 4, P])
            for i, ap in enumerate(sources):
                for u in range(2):
                    words = ap.bitcast(F32)[:, u : u + 2 * P - 1 : 2]
                    nc.tensor.transpose(t[:, 2 * i + u, :], words, ident[:])
            return t

        def flip_wc(g, half, engine):
            if half == 0:
                live["wc", g] = stage.tile([P, 4 * KVL], BF16, name="wc_stage%d" % g, tag="stage", bufs=6, align_bytes=64)
            t = flip4([wc_raw[half][:, e, 512 * g : 512 * g + 512] for e in range(2)])
            dst = live["wc", g][:].bitcast(F32).rearrange("q (e c u) -> q e c u", e=4, u=2)
            evac(engine, dst[:, 2 * half : 2 * half + 2], t[:].rearrange("q (e u) c -> q e c u", u=2))

        def quantise_wc(g):
            nc.vector.quantize_mx(
                out=wc_codes[:, g, :].bitcast(FP8X4), scales=wc_scales[:, g, :], in_=live["wc", g][:]
            )

        def flip_x(b, r, half, engine):
            if half == 0:
                live["x", b, r] = stage.tile([P, 4 * KVL], BF16, name="x_stage%d%d" % (b, r), tag="stage", bufs=6, align_bytes=64)
            t = flip4([x_raw[b][:, r, 512 * g : 512 * g + 512] for g in (2 * half, 2 * half + 1)])
            dst = live["x", b, r][:].bitcast(F32).rearrange("q (g c u) -> q g c u", g=G, u=2)
            evac(engine, dst[:, 2 * half : 2 * half + 2], t[:].rearrange("q (g u) c -> q g c u", u=2))

        def quantise_x(b, r):
            codes = small.tile([P, G, P], U32, name="x_codes%d%d" % (b, r), tag="x_codes", bufs=4, align_bytes=64)
            scales = small.tile([P, G, P], U8, name="x_scales%d%d" % (b, r), tag="x_scales", bufs=4, align_bytes=64)
            live["xq", b, r] = codes, scales
            nc.vector.quantize_mx(
                out=codes[:].rearrange("p g c -> p (g c)").bitcast(FP8X4),
                scales=scales[:].rearrange("p g c -> p (g c)"),
                in_=live["x", b, r][:],
            )

        def flip_wb(i, n, engine):
            if n == 0:
                live["wb", i] = stage.tile([P, 2 * Q, P * 4], BF16, name="wb_stage%d" % i, tag="wb_stage", bufs=2, align_bytes=64)
            t = flip4([wb_raw[i][:, 2 * n + e, :] for e in range(2)])
            dst = live["wb", i][:].rearrange("q m n -> q (m n)").bitcast(F32).rearrange("q (c n a) -> q c n a", c=P, a=4)
            evac(engine, dst[:, :, n], t[:].rearrange("q a c -> q c a"))

        def quantise_wb(i, v):
            for h in range(Q):
                cols = slice(P * h, P * h + P)
                nc.vector.quantize_mx(
                    out=wb_codes[:, i, v, cols].bitcast(FP8X4),
                    scales=wb_scales[:, i, v, cols],
                    in_=live["wb", i][:, 2 * h + v, :],
                )

        def stage1(b, r):
            acc = bank([P, 4, P])
            live["m1", b, r] = acc
            codes, scales = live["xq", b, r]
            for j in range(4):
                rows = slice(P * j, P * j + P)
                for g in range(G):
                    nc.tensor.matmul_mx(
                        out=acc[:, j, :],
                        lhsT=wc_codes[:, g, rows].bitcast(FP8X4),
                        lhsT_scale=wc_scales[:, g, rows],
                        rhs=codes[:, g, :].bitcast(FP8X4),
                        rhs_scale=scales[:, g, :],
                        start=(g == 0),
                        stop=(g == G - 1),
                    )

        def stage1_out(b, r, engine):
            kv = stage.tile([P, P, 4], BF16, name="kv%d%d" % (b, r), tag="kv", align_bytes=64)
            live["kv", b, r] = kv
            evac(engine, kv[:], live["m1", b, r][:].rearrange("q j t -> q t j"))

        def stage1_quantise(b, r):
            codes = small.tile([P, P], U32, name="kv_codes%d%d" % (b, r), tag="kv_codes", bufs=4, align_bytes=64)
            scales = small.tile([P, P], U8, name="kv_scales%d%d" % (b, r), tag="kv_scales", bufs=4, align_bytes=64)
            live["kvq", b, r] = codes, scales
            nc.vector.quantize_mx(
                out=codes[:].bitcast(FP8X4), scales=scales[:], in_=live["kv", b, r][:].rearrange("q t j -> q (t j)")
            )

        def product(b, r, v, i, engine):
            t = bank([P, 512])
            codes, scales = live["kvq", b, r]
            nc.tensor.matmul_mx(
                out=t[:],
                lhsT=codes[:].bitcast(FP8X4),
                lhsT_scale=scales[:],
                rhs=wb_codes[:, i, v, :].bitcast(FP8X4),
                rhs_scale=wb_scales[:, i, v, :],
                start=True,
                stop=True,
            )
            if ("out", b, v) not in live:
                live["out", b, v] = outs.tile([P, 2, H * P], F32, name="out%d%d" % (b, v), tag="out%d" % v, bufs=3 - v)
            dst = live["out", b, v][:, r, 512 * i : 512 * i + 512]
            if v == 0:
                nc.scalar.activation(out=dst, in_=t[:], func=ACT.Silu)
            else:
                evac(engine, dst, t[:])

        def part_max(b, r, half):
            if ("pm", b) not in live:
                live["pm", b] = small.tile([P, 4], F32, name="pm%d" % b, tag="pm")
            nc.vector.tensor_reduce(
                out=live["pm", b][:, 2 * r + half : 2 * r + half + 1],
                in_=live["out", b, 0][:, r, 1024 * half : 1024 * half + 1024],
                axis=AX.X,
                op=ALU.max,
            )

        def whole_max(b):
            tm = small.tile([P, 1], F32, name="tm%d" % b, tag="tm")
            nc.vector.tensor_reduce(out=tm[:], in_=live["pm", b][:], axis=AX.X, op=ALU.max)
            live["tm", b] = tm

        def flip_max(b):
            t = bank([P, 4, P])
            live["ft", b] = t
            nc.tensor.transpose(t[:, 0, :], live["tm", b][:].to_broadcast([P, P]), ident[:])

        def factors(b):
            m = small.tile([P, H], F32, name="m%d" % b, tag="m")
            nc.vector.tensor_reduce(
                out=m[:], in_=live["ft", b][:, 0, :].rearrange("q (g s) -> q g s", s=8), axis=AX.X, op=ALU.max
            )
            z = small.tile([P, H], F32, name="z%d" % b, tag="z")
            nc.vector.scalar_tensor_tensor(
                out=z[:], in0=m[:], scalar=0.0, in1=m[:], op0=ALU.is_equal, op1=ALU.add
            )
            rc = small.tile([P, H], F32, name="rc%d" % b, tag="rc")
            nc.vector.reciprocal(out=rc[:], in_=z[:])
            eta = small.tile([P, H], F32, name="eta%d" % b, tag="eta")
            nc.vector.tensor_scalar(
                out=eta[:], in0=rc[:], scalar1=10.0, scalar2=1.0, op0=ALU.mult, op1=ALU.min
            )
            live["eta", b] = eta

        def scale_head(b, h, engine):
            a = live["out", b, 0][:, :, P * h : P * h + P]
            eta = live["eta", b][:, h : h + 1]
            if engine == "g":
                nc.gpsimd.tensor_scalar(out=a, in0=a, scalar1=eta, scalar2=1.0, op0=ALU.mult, op1=ALU.mult)
            elif engine == "v":
                nc.vector.tensor_scalar(out=a, in0=a, scalar1=eta, scalar2=None, op0=ALU.mult)
            else:
                nc.scalar.activation(out=a, in_=a, func=ACT.Copy, scale=eta)

        def store_values(b, r, i0, n):
            cols = slice(512 * i0, 512 * (i0 + n))
            nc.sync.dma_start(out=v_view[b, :, r, cols], in_=live["out", b, 1][:, r, cols])

        def store_keys(b, i0, n):
            cols = slice(512 * i0, 512 * (i0 + n))
            nc.sync.dma_start(out=k_view[b, :, :, cols], in_=live["out", b, 0][:, :, cols])


        pending = []

        def later(lag, step):
            pending.append([lag, step])

        def flush():
            for entry in [e for e in pending if e[0] <= 0]:
                pending.remove(entry)
                entry[1]()

        def tick():
            for entry in pending:
                entry[0] -= 1
            flush()

        def do_wc(g, half, engine):
            flip_wc(g, half, engine)
            if half == 1:
                later(2, lambda: quantise_wc(g))
            tick()

        def do_x(b, r):
            for half in range(2):
                flip_x(b, r, half, ("svss" if b else "svsv")[2 * r + half])
                if half == 1:
                    later(1, lambda: quantise_x(b, r))
                tick()

        def do_wb(i):
            for n in range(4):
                flip_wb(i, n, "svss"[n])
                if n == 3:
                    later(2, lambda: quantise_wb(i, 0))
                    later(3, lambda: quantise_wb(i, 1))
                tick()

        def do_stage1(b, r):
            stage1(b, r)
            stage1_out(b, r, "sv"[r])
            later(1, lambda: stage1_quantise(b, r))
            tick()

        def do_keys(b, r, half):
            for i in (2 * half, 2 * half + 1):
                product(b, r, 0, i, "s")
                if i == 2 * half + 1:
                    later(1, lambda: part_max(b, r, half))
                    if r == 1 and half == 1:
                        later(1, lambda: whole_max(b))
                tick()

        def do_values(b, r, half):
            for i in (2 * half, 2 * half + 1):
                product(b, r, 1, i, ["ssssssss","ssssssss","ssssssss","ssssssvs"][b][4 * r + i])
                if 2 == 4 and i == 3:
                    later(1, lambda: store_values(b, r, 0, 4))
                elif 2 == 2 and i == 2 * half + 1:
                    later(1, lambda: store_values(b, r, 2 * half, 2))
                tick()

        def finish_keys(b):
            step = [0.5,0.5,0.5,0][b]
            klag = [[1,1],[1,1],[1,1],[0,0]][b]
            engines = ["v","v","v","vvs"][b]
            start = [1,1,1,0][b]
            flip_max(b)
            later(0, lambda: factors(b))
            for h in range(H):
                later(start + int(h * step), lambda h=h: scale_head(b, h, engines[h % len(engines)]))
                if b + 1 < B:
                    if h % (4 * 2) == 4 * 2 - 1:
                        later(start + int(h * step) + klag[h // 8], lambda h=h: store_keys(b, h // Q + 1 - 2, 2))
                elif h % 4 == 3:
                    later(start + int(h * step), lambda h=h: store_keys(b, h // Q, 1))
            flush()

        patterns = ["xxwwwwwwwwWMMWLWLWKKKKXXVVFVMMVX","KKKKVXVVFMVMX","KKKKVXVVFMVM","KKKKVVVFV"]
        ahead = dict(X=0, M=0, W=0, x=0, w=0)
        for b in range(B):
            count = dict(L=0, K=0, V=0)
            for step in patterns[b]:
                n = ahead[step] if step in ahead else count.get(step)
                if step == "x":
                    do_x(0, n)
                elif step == "w":
                    do_wc(n % G, n // G, "sv"[n % 2])
                elif step == "W":
                    do_wb(n)
                elif step == "K":
                    do_keys(b, n // 2, n % 2)
                elif step == "V":
                    do_values(b, n // 2, n % 2)
                elif step == "L":
                    load_x(len(x_raw))
                elif step == "X":
                    do_x(1 + n // 2, n % 2)
                elif step == "M":
                    do_stage1(n // 2, n % 2)
                else:
                    finish_keys(b)
                if step in ahead:
                    ahead[step] += 1
                elif step != "F":
                    count[step] += 1
        while pending:
            tick()
